import numpy as np
import ml_dtypes

BF16 = ml_dtypes.bfloat16


def bf(x):
    return np.asarray(x, np.float32).astype(BF16)


def f32(x):
    return np.asarray(x, np.float32)


def f64(x):
    return np.asarray(x).astype(np.float64)


def striped(idx):
    return np.tile(idx.reshape(-1, 16).T, (8, 1))


C, S, H, K, N = 512, 512, 256, 8, 2048
EPS = 1e-5


def setup_inputs():
    spread = 0.5 + np.random.random((1, S))
    shift = 0.5 * np.random.standard_normal((1, S))
    emb = f32(spread * np.random.standard_normal((C, S)) + shift)
    gain = f32(1.0 + 0.1 * np.random.standard_normal((C, 1)))
    idx = np.concatenate([np.random.permutation(S)[:H] for _ in range(K)])
    return {"emb": emb, "gain": gain, "offs": striped(idx)}


def reference(emb, gain, offs):
    idx = offs[:16].T.reshape(-1)
    e = f64(emb)
    mean = e.mean(axis=0, keepdims=True)
    var = ((e - mean) ** 2).mean(axis=0, keepdims=True)
    z = (e - mean) / np.sqrt(var + EPS)
    return z[:, idx] * f64(gain)

@@ -1,0 +1,74 @@
+import concourse.mybir as mybir
+
+F32 = mybir.dt.float32
+U16 = mybir.dt.uint16
+ALU = mybir.AluOpType
+FUNC = mybir.ActivationFunctionType
+
+P = 128
+C, S, N = 512, 512, 2048
+BLOCKS = C // P
+PIECE = 512
+EPS = 1e-5
+
+
+def tile_ctcliptext_kernel(tc, emb, gain, offs, out):
+    nc = tc.nc
+    emb_blocks = emb.rearrange("(p b) s -> p b s", b=BLOCKS)
+    out_blocks = out.rearrange("(p b) n -> p b n", b=BLOCKS)
+    gain_blocks = gain.rearrange("(p b) o -> p (b o)", b=BLOCKS)
+
+    with (
+        tc.tile_pool(name="held", bufs=1) as held,
+        tc.tile_pool(name="staged", bufs=8) as staged,
+        tc.psum_pool(name="psum", bufs=1) as psum,
+    ):
+        raw = [held.tile([P, S], F32, name=f"raw{b}") for b in range(BLOCKS)]
+        for b in range(BLOCKS):
+            queue = nc.sync if b % 2 == 0 else nc.scalar
+            queue.dma_start(raw[b][:], emb_blocks[:, b, :])
+        offsets = held.tile([P, N // 16], U16, name="offsets")
+        nc.sync.dma_start(offsets[:], offs)
+        gains = held.tile([P, BLOCKS], F32, name="gains")
+        nc.gpsimd.dma_start(gains[:], gain_blocks)
+        gain_wide = [held.tile([P, PIECE], F32, name=f"gain_wide{b}") for b in range(BLOCKS)]
+        for b in range(BLOCKS):
+            nc.gpsimd.tensor_copy(gain_wide[b][:], gains[:, b : b + 1].to_broadcast([P, PIECE]))
+
+        averager = held.tile([P, P], F32, name="averager")
+        nc.vector.memset(averager[:], 1.0 / C)
+        eps = held.tile([P, 1], F32, name="eps")
+        nc.vector.memset(eps[:], EPS)
+        warm = held.tile([P, 1], F32, name="warm")
+        nc.scalar.activation(warm[:], eps[:], FUNC.Abs_reciprocal_sqrt)
+
+        mean = psum.tile([P, S], F32, name="mean")
+        for b in range(BLOCKS):
+            nc.tensor.matmul(mean[:], averager[:], raw[b][:], start=(b == 0), stop=(b == BLOCKS - 1))
+
+        centred = [held.tile([P, S], F32, name=f"centred{b}") for b in range(BLOCKS)]
+        squared = [held.tile([P, S], F32, name=f"squared{b}") for b in range(BLOCKS)]
+        var = psum.tile([P, S], F32, name="var")
+        for b in range(BLOCKS):
+            nc.vector.tensor_tensor(centred[b][:], raw[b][:], mean[:], ALU.subtract)
+            nc.scalar.activation(squared[b][:], centred[b][:], FUNC.Square)
+            nc.tensor.matmul(var[:], averager[:], squared[b][:], start=(b == 0), stop=(b == BLOCKS - 1))
+        rstd = held.tile([P, S], F32, name="rstd")
+        nc.scalar.activation(rstd[:], var[:], FUNC.Abs_reciprocal_sqrt, bias=eps[:])
+
+        z = [held.tile([P, S], F32, name=f"z{b}") for b in range(BLOCKS)]
+        for b in range(BLOCKS):
+            engine = nc.vector if b == 0 else nc.gpsimd
+            engine.tensor_tensor(z[b][:], centred[b][:], rstd[:], ALU.mult)
+
+        for b in range(BLOCKS):
+            for k in range(N // PIECE):
+                picked = staged.tile([P, PIECE], F32, name="picked")
+                nc.vector.tensor_tensor(
+                    picked[:],
+                    z[b][:].indirect(offsets[:, k * (PIECE // 16) : (k + 1) * (PIECE // 16)]),
+                    gain_wide[b][:],
+                    ALU.mult,
+                )
+                queue = nc.sync if k % 2 == 0 else nc.scalar
+                queue.dma_start(out_blocks[:, b, k * PIECE : (k + 1) * PIECE], picked[:])

@@ -43,8 +43,10 @@ def tile_ctcliptext_kernel(tc, emb, gain, offs, out):
         nc.scalar.activation(warm[:], eps[:], FUNC.Abs_reciprocal_sqrt)
 
         mean = psum.tile([P, S], F32, name="mean")
-        for b in range(BLOCKS):
-            nc.tensor.matmul(mean[:], averager[:], raw[b][:], start=(b == 0), stop=(b == BLOCKS - 1))
+        for h in range(2):
+            raw_pair = held.tile([P, S], F32, name=f"raw_pair{h}")
+            nc.vector.tensor_tensor(raw_pair[:], raw[2 * h][:], raw[2 * h + 1][:], ALU.add)
+            nc.tensor.matmul(mean[:], averager[:], raw_pair[:], start=(h == 0), stop=(h == 1))
 
         centred = [held.tile([P, S], F32, name=f"centred{b}") for b in range(BLOCKS)]
         squared = [held.tile([P, S], F32, name=f"squared{b}") for b in range(BLOCKS)]
@@ -52,7 +54,11 @@ def tile_ctcliptext_kernel(tc, emb, gain, offs, out):
         for b in range(BLOCKS):
             nc.vector.tensor_tensor(centred[b][:], raw[b][:], mean[:], ALU.subtract)
             nc.scalar.activation(squared[b][:], centred[b][:], FUNC.Square)
-            nc.tensor.matmul(var[:], averager[:], squared[b][:], start=(b == 0), stop=(b == BLOCKS - 1))
+        nc.tensor.matmul(var[:], averager[:], squared[0][:], start=True, stop=False)
+        nc.tensor.matmul(var[:], averager[:], squared[1][:], start=False, stop=False)
+        squared_pair = held.tile([P, S], F32, name="squared_pair")
+        nc.vector.tensor_tensor(squared_pair[:], squared[2][:], squared[3][:], ALU.add)
+        nc.tensor.matmul(var[:], averager[:], squared_pair[:], start=False, stop=True)
         rstd = held.tile([P, S], F32, name="rstd")
         nc.scalar.activation(rstd[:], var[:], FUNC.Abs_reciprocal_sqrt, bias=eps[:])
 

@@ -1,4 +1,5 @@
 import concourse.mybir as mybir
+from concourse.masks import make_identity
 
 F32 = mybir.dt.float32
 U16 = mybir.dt.uint16
@@ -8,6 +9,7 @@ FUNC = mybir.ActivationFunctionType
 P = 128
 C, S, N = 512, 512, 2048
 BLOCKS = C // P
+WORD_BLOCKS = S // P
 PIECE = 512
 EPS = 1e-5
 
@@ -21,51 +23,51 @@ def tile_ctcliptext_kernel(tc, emb, gain, offs, out):
     with (
         tc.tile_pool(name="held", bufs=1) as held,
         tc.tile_pool(name="staged", bufs=8) as staged,
-        tc.psum_pool(name="psum", bufs=1) as psum,
+        tc.psum_pool(name="flipped", bufs=1) as flipped,
+        tc.psum_pool(name="back", bufs=2) as back,
     ):
-        raw = [held.tile([P, S], F32, name=f"raw{b}") for b in range(BLOCKS)]
-        for b in range(BLOCKS):
-            queue = nc.sync if b % 2 == 0 else nc.scalar
-            queue.dma_start(raw[b][:], emb_blocks[:, b, :])
+        raw = [held.tile([P, BLOCKS, P], F32, name=f"raw{w}") for w in range(WORD_BLOCKS)]
+        for w in range(WORD_BLOCKS):
+            queue = nc.sync if w % 2 == 0 else nc.scalar
+            queue.dma_start(raw[w][:], emb_blocks[:, :, w * P : (w + 1) * P])
         offsets = held.tile([P, N // 16], U16, name="offsets")
         nc.sync.dma_start(offsets[:], offs)
         gains = held.tile([P, BLOCKS], F32, name="gains")
         nc.gpsimd.dma_start(gains[:], gain_blocks)
+
+        identity = held.tile([P, P], F32, name="identity")
+        make_identity(nc, identity[:])
+        eps = held.tile([P, 1], F32, name="eps")
+        nc.vector.memset(eps[:], EPS)
+        warm = held.tile([P, 1], F32, name="warm")
+        nc.scalar.activation(warm[:], eps[:], FUNC.Sqrt)
         gain_wide = [held.tile([P, PIECE], F32, name=f"gain_wide{b}") for b in range(BLOCKS)]
         for b in range(BLOCKS):
             nc.gpsimd.tensor_copy(gain_wide[b][:], gains[:, b : b + 1].to_broadcast([P, PIECE]))
 
-        averager = held.tile([P, P], F32, name="averager")
-        nc.vector.memset(averager[:], 1.0 / C)
-        eps = held.tile([P, 1], F32, name="eps")
-        nc.vector.memset(eps[:], EPS)
-        warm = held.tile([P, 1], F32, name="warm")
-        nc.scalar.activation(warm[:], eps[:], FUNC.Abs_reciprocal_sqrt)
-
-        mean = psum.tile([P, S], F32, name="mean")
-        for h in range(2):
-            raw_pair = held.tile([P, S], F32, name=f"raw_pair{h}")
-            nc.vector.tensor_tensor(raw_pair[:], raw[2 * h][:], raw[2 * h + 1][:], ALU.add)
-            nc.tensor.matmul(mean[:], averager[:], raw_pair[:], start=(h == 0), stop=(h == 1))
-
-        centred = [held.tile([P, S], F32, name=f"centred{b}") for b in range(BLOCKS)]
-        squared = [held.tile([P, S], F32, name=f"squared{b}") for b in range(BLOCKS)]
-        var = psum.tile([P, S], F32, name="var")
-        for b in range(BLOCKS):
-            nc.vector.tensor_tensor(centred[b][:], raw[b][:], mean[:], ALU.subtract)
-            nc.scalar.activation(squared[b][:], centred[b][:], FUNC.Square)
-        nc.tensor.matmul(var[:], averager[:], squared[0][:], start=True, stop=False)
-        nc.tensor.matmul(var[:], averager[:], squared[1][:], start=False, stop=False)
-        squared_pair = held.tile([P, S], F32, name="squared_pair")
-        nc.vector.tensor_tensor(squared_pair[:], squared[2][:], squared[3][:], ALU.add)
-        nc.tensor.matmul(var[:], averager[:], squared_pair[:], start=False, stop=True)
-        rstd = held.tile([P, S], F32, name="rstd")
-        nc.scalar.activation(rstd[:], var[:], FUNC.Abs_reciprocal_sqrt, bias=eps[:])
+        z_flipped = [held.tile([P, C], F32, name=f"z_flipped{w}") for w in range(WORD_BLOCKS)]
+        for w in range(WORD_BLOCKS):
+            raw_flipped = flipped.tile([P, C], F32, name=f"raw_flipped{w}")
+            for b in range(BLOCKS):
+                nc.tensor.transpose(raw_flipped[:, b * P : (b + 1) * P], raw[w][:, b, :], identity[:])
+            stats = held.tile([P, 6], F32, name=f"stats{w}")
+            nc.vector.bn_stats(stats[:], raw_flipped[:])
+            mean_var = held.tile([P, 2], F32, name=f"mean_var{w}")
+            nc.vector.bn_aggr(mean_var[:], stats[:])
+            std = held.tile([P, 1], F32, name=f"std{w}")
+            nc.scalar.activation(std[:], mean_var[:, 1:2], FUNC.Sqrt, bias=eps[:])
+            rstd = held.tile([P, 1], F32, name=f"rstd{w}")
+            nc.vector.reciprocal(rstd[:], std[:])
+            shift = held.tile([P, 1], F32, name=f"shift{w}")
+            nc.vector.tensor_scalar(shift[:], mean_var[:, 0:1], rstd[:], -1.0, ALU.mult, ALU.mult)
+            nc.scalar.activation(z_flipped[w][:], raw_flipped[:], FUNC.Identity, bias=shift[:], scale=rstd[:])
 
         z = [held.tile([P, S], F32, name=f"z{b}") for b in range(BLOCKS)]
         for b in range(BLOCKS):
-            engine = nc.vector if b == 0 else nc.gpsimd
-            engine.tensor_tensor(z[b][:], centred[b][:], rstd[:], ALU.mult)
+            z_psum = back.tile([P, S], F32, name="z_psum")
+            for w in range(WORD_BLOCKS):
+                nc.tensor.transpose(z_psum[:, w * P : (w + 1) * P], z_flipped[w][:, b * P : (b + 1) * P], identity[:])
+            nc.scalar.copy(z[b][:], z_psum[:])
 
         for b in range(BLOCKS):
             for k in range(N // PIECE):

@@ -45,28 +45,47 @@ def tile_ctcliptext_kernel(tc, emb, gain, offs, out):
         for b in range(BLOCKS):
             nc.gpsimd.tensor_copy(gain_wide[b][:], gains[:, b : b + 1].to_broadcast([P, PIECE]))
 
-        z_flipped = [held.tile([P, C], F32, name=f"z_flipped{w}") for w in range(WORD_BLOCKS)]
+        raw_flipped = [flipped.tile([P, C], F32, name=f"raw_flipped{w}") for w in range(WORD_BLOCKS)]
         for w in range(WORD_BLOCKS):
-            raw_flipped = flipped.tile([P, C], F32, name=f"raw_flipped{w}")
             for b in range(BLOCKS):
-                nc.tensor.transpose(raw_flipped[:, b * P : (b + 1) * P], raw[w][:, b, :], identity[:])
-            stats = held.tile([P, 6], F32, name=f"stats{w}")
-            nc.vector.bn_stats(stats[:], raw_flipped[:])
-            mean_var = held.tile([P, 2], F32, name=f"mean_var{w}")
-            nc.vector.bn_aggr(mean_var[:], stats[:])
-            std = held.tile([P, 1], F32, name=f"std{w}")
-            nc.scalar.activation(std[:], mean_var[:, 1:2], FUNC.Sqrt, bias=eps[:])
-            rstd = held.tile([P, 1], F32, name=f"rstd{w}")
-            nc.vector.reciprocal(rstd[:], std[:])
-            shift = held.tile([P, 1], F32, name=f"shift{w}")
-            nc.vector.tensor_scalar(shift[:], mean_var[:, 0:1], rstd[:], -1.0, ALU.mult, ALU.mult)
-            nc.scalar.activation(z_flipped[w][:], raw_flipped[:], FUNC.Identity, bias=shift[:], scale=rstd[:])
+                nc.tensor.transpose(raw_flipped[w][:, b * P : (b + 1) * P], raw[w][:, b, :], identity[:])
+
+        stats = held.tile([P, WORD_BLOCKS, 6], F32, name="stats")
+        mean_var = held.tile([P, WORD_BLOCKS, 2], F32, name="mean_var")
+        for w in range(WORD_BLOCKS):
+            nc.vector.bn_stats(stats[:, w, :], raw_flipped[w][:])
+            if w > 0:
+                nc.vector.bn_aggr(mean_var[:, w - 1, :], stats[:, w - 1, :])
+        nc.vector.bn_aggr(mean_var[:, WORD_BLOCKS - 1, :], stats[:, WORD_BLOCKS - 1, :])
+        std = held.tile([P, WORD_BLOCKS], F32, name="std")
+        nc.scalar.activation(std[:], mean_var[:, :, 1], FUNC.Sqrt, bias=eps[:])
+        rstd = held.tile([P, WORD_BLOCKS], F32, name="rstd")
+        nc.vector.reciprocal(rstd[:], std[:])
 
         z = [held.tile([P, S], F32, name=f"z{b}") for b in range(BLOCKS)]
-        for b in range(BLOCKS):
+
+        first_flipped = held.tile([P, WORD_BLOCKS, P], F32, name="first_flipped")
+        first_psum = back.tile([P, S], F32, name="z_psum")
+        for w in range(WORD_BLOCKS):
+            nc.vector.tensor_scalar(
+                first_flipped[:, w, :], raw_flipped[w][:, 0:P],
+                mean_var[:, w, 0:1], rstd[:, w : w + 1], ALU.subtract, ALU.mult,
+            )
+            nc.tensor.transpose(first_psum[:, w * P : (w + 1) * P], first_flipped[:, w, :], identity[:])
+        shift = held.tile([P, WORD_BLOCKS], F32, name="shift")
+        nc.vector.scalar_tensor_tensor(shift[:], mean_var[:, :, 0], -1.0, rstd[:], ALU.mult, ALU.mult)
+        nc.vector.tensor_copy(z[0][:], first_psum[:])
+
+        rest_flipped = [held.tile([P, C - P], F32, name=f"rest_flipped{w}") for w in range(WORD_BLOCKS)]
+        for w in range(WORD_BLOCKS):
+            nc.scalar.activation(
+                rest_flipped[w][:], raw_flipped[w][:, P:C], FUNC.Identity,
+                bias=shift[:, w : w + 1], scale=rstd[:, w : w + 1],
+            )
+        for b in range(1, BLOCKS):
             z_psum = back.tile([P, S], F32, name="z_psum")
             for w in range(WORD_BLOCKS):
-                nc.tensor.transpose(z_psum[:, w * P : (w + 1) * P], z_flipped[w][:, b * P : (b + 1) * P], identity[:])
+                nc.tensor.transpose(z_psum[:, w * P : (w + 1) * P], rest_flipped[w][:, (b - 1) * P : b * P], identity[:])
             nc.scalar.copy(z[b][:], z_psum[:])
 
         for b in range(BLOCKS):

@@ -12,6 +12,7 @@ BLOCKS = C // P
 WORD_BLOCKS = S // P
 PIECE = 512
 EPS = 1e-5
+WARM_UPS = 4
 
 
 def tile_ctcliptext_kernel(tc, emb, gain, offs, out):
@@ -25,6 +26,7 @@ def tile_ctcliptext_kernel(tc, emb, gain, offs, out):
         tc.tile_pool(name="staged", bufs=8) as staged,
         tc.psum_pool(name="flipped", bufs=1) as flipped,
         tc.psum_pool(name="back", bufs=2) as back,
+        tc.psum_pool(name="spare", bufs=1) as spare,
     ):
         raw = [held.tile([P, BLOCKS, P], F32, name=f"raw{w}") for w in range(WORD_BLOCKS)]
         for w in range(WORD_BLOCKS):
@@ -37,6 +39,11 @@ def tile_ctcliptext_kernel(tc, emb, gain, offs, out):
 
         identity = held.tile([P, P], F32, name="identity")
         make_identity(nc, identity[:])
+        filler = held.tile([P, P], F32, name="filler")
+        nc.vector.memset(filler[:], 0.0)
+        unused = spare.tile([P, P], F32, name="unused")
+        for i in range(WARM_UPS):
+            nc.tensor.matmul(unused[:], filler[:], filler[:], start=True, stop=True)
         eps = held.tile([P, 1], F32, name="eps")
         nc.vector.memset(eps[:], EPS)
         warm = held.tile([P, 1], F32, name="warm")

@@ -10,9 +10,8 @@ P = 128
 C, S, N = 512, 512, 2048
 BLOCKS = C // P
 WORD_BLOCKS = S // P
-PIECE = 512
+PIECE = S
 EPS = 1e-5
-WARM_UPS = 4
 
 
 def tile_ctcliptext_kernel(tc, emb, gain, offs, out):
@@ -26,7 +25,6 @@ def tile_ctcliptext_kernel(tc, emb, gain, offs, out):
         tc.tile_pool(name="staged", bufs=8) as staged,
         tc.psum_pool(name="flipped", bufs=1) as flipped,
         tc.psum_pool(name="back", bufs=2) as back,
-        tc.psum_pool(name="spare", bufs=1) as spare,
     ):
         raw = [held.tile([P, BLOCKS, P], F32, name=f"raw{w}") for w in range(WORD_BLOCKS)]
         for w in range(WORD_BLOCKS):
@@ -39,15 +37,8 @@ def tile_ctcliptext_kernel(tc, emb, gain, offs, out):
 
         identity = held.tile([P, P], F32, name="identity")
         make_identity(nc, identity[:])
-        filler = held.tile([P, P], F32, name="filler")
-        nc.vector.memset(filler[:], 0.0)
-        unused = spare.tile([P, P], F32, name="unused")
-        for i in range(WARM_UPS):
-            nc.tensor.matmul(unused[:], filler[:], filler[:], start=True, stop=True)
         eps = held.tile([P, 1], F32, name="eps")
         nc.vector.memset(eps[:], EPS)
-        warm = held.tile([P, 1], F32, name="warm")
-        nc.scalar.activation(warm[:], eps[:], FUNC.Sqrt)
         gain_wide = [held.tile([P, PIECE], F32, name=f"gain_wide{b}") for b in range(BLOCKS)]
         for b in range(BLOCKS):
             nc.gpsimd.tensor_copy(gain_wide[b][:], gains[:, b : b + 1].to_broadcast([P, PIECE]))
@@ -61,9 +52,7 @@ def tile_ctcliptext_kernel(tc, emb, gain, offs, out):
         mean_var = held.tile([P, WORD_BLOCKS, 2], F32, name="mean_var")
         for w in range(WORD_BLOCKS):
             nc.vector.bn_stats(stats[:, w, :], raw_flipped[w][:])
-            if w > 0:
-                nc.vector.bn_aggr(mean_var[:, w - 1, :], stats[:, w - 1, :])
-        nc.vector.bn_aggr(mean_var[:, WORD_BLOCKS - 1, :], stats[:, WORD_BLOCKS - 1, :])
+            nc.vector.bn_aggr(mean_var[:, w, :], stats[:, w, :])
         std = held.tile([P, WORD_BLOCKS], F32, name="std")
         nc.scalar.activation(std[:], mean_var[:, :, 1], FUNC.Sqrt, bias=eps[:])
         rstd = held.tile([P, WORD_BLOCKS], F32, name="rstd")
@@ -72,16 +61,16 @@ def tile_ctcliptext_kernel(tc, emb, gain, offs, out):
         z = [held.tile([P, S], F32, name=f"z{b}") for b in range(BLOCKS)]
 
         first_flipped = held.tile([P, WORD_BLOCKS, P], F32, name="first_flipped")
-        first_psum = back.tile([P, S], F32, name="z_psum")
+        z_psum = back.tile([P, S], F32, name="z_psum")
         for w in range(WORD_BLOCKS):
             nc.vector.tensor_scalar(
                 first_flipped[:, w, :], raw_flipped[w][:, 0:P],
                 mean_var[:, w, 0:1], rstd[:, w : w + 1], ALU.subtract, ALU.mult,
             )
-            nc.tensor.transpose(first_psum[:, w * P : (w + 1) * P], first_flipped[:, w, :], identity[:])
+            nc.tensor.transpose(z_psum[:, w * P : (w + 1) * P], first_flipped[:, w, :], identity[:])
         shift = held.tile([P, WORD_BLOCKS], F32, name="shift")
         nc.vector.scalar_tensor_tensor(shift[:], mean_var[:, :, 0], -1.0, rstd[:], ALU.mult, ALU.mult)
-        nc.vector.tensor_copy(z[0][:], first_psum[:])
+        nc.vector.tensor_copy(z[0][:], z_psum[:])
 
         rest_flipped = [held.tile([P, C - P], F32, name=f"rest_flipped{w}") for w in range(WORD_BLOCKS)]
         for w in range(WORD_BLOCKS):

@@ -24,6 +24,7 @@ def tile_ctcliptext_kernel(tc, emb, gain, offs, out):
         tc.tile_pool(name="held", bufs=1) as held,
         tc.tile_pool(name="staged", bufs=8) as staged,
         tc.psum_pool(name="flipped", bufs=1) as flipped,
+        tc.psum_pool(name="first", bufs=1) as first,
         tc.psum_pool(name="back", bufs=2) as back,
     ):
         raw = [held.tile([P, BLOCKS, P], F32, name=f"raw{w}") for w in range(WORD_BLOCKS)]
@@ -50,27 +51,33 @@ def tile_ctcliptext_kernel(tc, emb, gain, offs, out):
 
         stats = held.tile([P, WORD_BLOCKS, 6], F32, name="stats")
         mean_var = held.tile([P, WORD_BLOCKS, 2], F32, name="mean_var")
-        for w in range(WORD_BLOCKS):
+        rstd = held.tile([P, WORD_BLOCKS], F32, name="rstd")
+
+        def measure(w):
             nc.vector.bn_stats(stats[:, w, :], raw_flipped[w][:])
             nc.vector.bn_aggr(mean_var[:, w, :], stats[:, w, :])
-        std = held.tile([P, WORD_BLOCKS], F32, name="std")
-        nc.scalar.activation(std[:], mean_var[:, :, 1], FUNC.Sqrt, bias=eps[:])
-        rstd = held.tile([P, WORD_BLOCKS], F32, name="rstd")
-        nc.vector.reciprocal(rstd[:], std[:])
+            nc.scalar.activation(rstd[:, w : w + 1], mean_var[:, w, 1:2], FUNC.Abs_reciprocal_sqrt, bias=eps[:])
 
         z = [held.tile([P, S], F32, name=f"z{b}") for b in range(BLOCKS)]
 
         first_flipped = held.tile([P, WORD_BLOCKS, P], F32, name="first_flipped")
-        z_psum = back.tile([P, S], F32, name="z_psum")
-        for w in range(WORD_BLOCKS):
+        first_psum = first.tile([P, S], F32, name="first_psum")
+
+        def normalise_first(w):
             nc.vector.tensor_scalar(
                 first_flipped[:, w, :], raw_flipped[w][:, 0:P],
                 mean_var[:, w, 0:1], rstd[:, w : w + 1], ALU.subtract, ALU.mult,
             )
-            nc.tensor.transpose(z_psum[:, w * P : (w + 1) * P], first_flipped[:, w, :], identity[:])
+            nc.tensor.transpose(first_psum[:, w * P : (w + 1) * P], first_flipped[:, w, :], identity[:])
+
+        measure(0)
+        for w in range(1, WORD_BLOCKS):
+            measure(w)
+            normalise_first(w - 1)
+        normalise_first(WORD_BLOCKS - 1)
         shift = held.tile([P, WORD_BLOCKS], F32, name="shift")
         nc.vector.scalar_tensor_tensor(shift[:], mean_var[:, :, 0], -1.0, rstd[:], ALU.mult, ALU.mult)
-        nc.vector.tensor_copy(z[0][:], z_psum[:])
+        nc.vector.tensor_copy(z[0][:], first_psum[:])
 
         rest_flipped = [held.tile([P, C - P], F32, name=f"rest_flipped{w}") for w in range(WORD_BLOCKS)]
         for w in range(WORD_BLOCKS):

@@ -11,6 +11,7 @@ C, S, N = 512, 512, 2048
 BLOCKS = C // P
 WORD_BLOCKS = S // P
 PIECE = S
+LAST_PIECE = 128
 EPS = 1e-5
 
 
@@ -29,8 +30,7 @@ def tile_ctcliptext_kernel(tc, emb, gain, offs, out):
     ):
         raw = [held.tile([P, BLOCKS, P], F32, name=f"raw{w}") for w in range(WORD_BLOCKS)]
         for w in range(WORD_BLOCKS):
-            queue = nc.sync if w % 2 == 0 else nc.scalar
-            queue.dma_start(raw[w][:], emb_blocks[:, :, w * P : (w + 1) * P])
+            nc.sync.dma_start(raw[w][:], emb_blocks[:, :, w * P : (w + 1) * P])
         offsets = held.tile([P, N // 16], U16, name="offsets")
         nc.sync.dma_start(offsets[:], offs)
         gains = held.tile([P, BLOCKS], F32, name="gains")
@@ -61,14 +61,17 @@ def tile_ctcliptext_kernel(tc, emb, gain, offs, out):
         z = [held.tile([P, S], F32, name=f"z{b}") for b in range(BLOCKS)]
 
         first_flipped = held.tile([P, WORD_BLOCKS, P], F32, name="first_flipped")
-        first_psum = first.tile([P, S], F32, name="first_psum")
+        EARLY = (WORD_BLOCKS - 1) * P
+        early_psum = first.tile([P, EARLY], F32, name="early_psum")
+        last_psum = first.tile([P, P], F32, name="last_psum")
 
         def normalise_first(w):
             nc.vector.tensor_scalar(
                 first_flipped[:, w, :], raw_flipped[w][:, 0:P],
                 mean_var[:, w, 0:1], rstd[:, w : w + 1], ALU.subtract, ALU.mult,
             )
-            nc.tensor.transpose(first_psum[:, w * P : (w + 1) * P], first_flipped[:, w, :], identity[:])
+            back_in_psum = early_psum[:, w * P : (w + 1) * P] if w < WORD_BLOCKS - 1 else last_psum[:]
+            nc.tensor.transpose(back_in_psum, first_flipped[:, w, :], identity[:])
 
         measure(0)
         for w in range(1, WORD_BLOCKS):
@@ -77,7 +80,8 @@ def tile_ctcliptext_kernel(tc, emb, gain, offs, out):
         normalise_first(WORD_BLOCKS - 1)
         shift = held.tile([P, WORD_BLOCKS], F32, name="shift")
         nc.vector.scalar_tensor_tensor(shift[:], mean_var[:, :, 0], -1.0, rstd[:], ALU.mult, ALU.mult)
-        nc.vector.tensor_copy(z[0][:], first_psum[:])
+        nc.vector.tensor_copy(z[0][:, 0:EARLY], early_psum[:])
+        nc.vector.tensor_copy(z[0][:, EARLY:S], last_psum[:])
 
         rest_flipped = [held.tile([P, C - P], F32, name=f"rest_flipped{w}") for w in range(WORD_BLOCKS)]
         for w in range(WORD_BLOCKS):
@@ -92,13 +96,17 @@ def tile_ctcliptext_kernel(tc, emb, gain, offs, out):
             nc.scalar.copy(z[b][:], z_psum[:])
 
         for b in range(BLOCKS):
-            for k in range(N // PIECE):
+            cuts = list(range(0, N + 1, PIECE))
+            if b == BLOCKS - 1:
+                cuts.insert(len(cuts) - 1, N - LAST_PIECE)
+            for k in range(len(cuts) - 1):
+                start, width = cuts[k], cuts[k + 1] - cuts[k]
                 picked = staged.tile([P, PIECE], F32, name="picked")
                 nc.vector.tensor_tensor(
-                    picked[:],
-                    z[b][:].indirect(offsets[:, k * (PIECE // 16) : (k + 1) * (PIECE // 16)]),
-                    gain_wide[b][:],
+                    picked[:, 0:width],
+                    z[b][:].indirect(offsets[:, start // 16 : (start + width) // 16]),
+                    gain_wide[b][:, 0:width],
                     ALU.mult,
                 )
                 queue = nc.sync if k % 2 == 0 else nc.scalar
-                queue.dma_start(out_blocks[:, b, k * PIECE : (k + 1) * PIECE], picked[:])
+                queue.dma_start(out_blocks[:, b, start : start + width], picked[:, 0:width])

@@ -34,7 +34,7 @@ def tile_ctcliptext_kernel(tc, emb, gain, offs, out):
         offsets = held.tile([P, N // 16], U16, name="offsets")
         nc.sync.dma_start(offsets[:], offs)
         gains = held.tile([P, BLOCKS], F32, name="gains")
-        nc.gpsimd.dma_start(gains[:], gain_blocks)
+        nc.scalar.dma_start(gains[:], gain_blocks)
 
         identity = held.tile([P, P], F32, name="identity")
         make_identity(nc, identity[:])
@@ -42,7 +42,7 @@ def tile_ctcliptext_kernel(tc, emb, gain, offs, out):
         nc.vector.memset(eps[:], EPS)
         gain_wide = [held.tile([P, PIECE], F32, name=f"gain_wide{b}") for b in range(BLOCKS)]
         for b in range(BLOCKS):
-            nc.gpsimd.tensor_copy(gain_wide[b][:], gains[:, b : b + 1].to_broadcast([P, PIECE]))
+            nc.vector.tensor_copy(gain_wide[b][:], gains[:, b : b + 1].to_broadcast([P, PIECE]))
 
         raw_flipped = [flipped.tile([P, C], F32, name=f"raw_flipped{w}") for w in range(WORD_BLOCKS)]
         for w in range(WORD_BLOCKS):

@@ -108,5 +108,4 @@ def tile_ctcliptext_kernel(tc, emb, gain, offs, out):
                     gain_wide[b][:, 0:width],
                     ALU.mult,
                 )
-                queue = nc.sync if k % 2 == 0 else nc.scalar
-                queue.dma_start(out_blocks[:, b, start : start + width], picked[:, 0:width])
+                nc.sync.dma_start(out_blocks[:, b, start : start + width], picked[:, 0:width])

@@ -23,7 +23,7 @@ def tile_ctcliptext_kernel(tc, emb, gain, offs, out):
 
     with (
         tc.tile_pool(name="held", bufs=1) as held,
-        tc.tile_pool(name="staged", bufs=8) as staged,
+        tc.tile_pool(name="staged", bufs=BLOCKS * (N // PIECE) + 1) as staged,
         tc.psum_pool(name="flipped", bufs=1) as flipped,
         tc.psum_pool(name="first", bufs=1) as first,
         tc.psum_pool(name="back", bufs=2) as back,

@@ -40,9 +40,11 @@ def tile_ctcliptext_kernel(tc, emb, gain, offs, out):
         make_identity(nc, identity[:])
         eps = held.tile([P, 1], F32, name="eps")
         nc.vector.memset(eps[:], EPS)
+        scratch = held.tile([P, 1], F32, name="scratch")
+        nc.scalar.activation(scratch[:], eps[:], FUNC.Abs_reciprocal_sqrt)
         gain_wide = [held.tile([P, PIECE], F32, name=f"gain_wide{b}") for b in range(BLOCKS)]
         for b in range(BLOCKS):
-            nc.vector.tensor_copy(gain_wide[b][:], gains[:, b : b + 1].to_broadcast([P, PIECE]))
+            nc.scalar.copy(gain_wide[b][:], gains[:, b : b + 1].to_broadcast([P, PIECE]))
 
         raw_flipped = [flipped.tile([P, C], F32, name=f"raw_flipped{w}") for w in range(WORD_BLOCKS)]
         for w in range(WORD_BLOCKS):

import concourse.mybir as mybir
from concourse.masks import make_identity

F32 = mybir.dt.float32
U16 = mybir.dt.uint16
ALU = mybir.AluOpType
FUNC = mybir.ActivationFunctionType

P = 128
C, S, N = 512, 512, 2048
BLOCKS = C // P
WORD_BLOCKS = S // P
PIECE = S
LAST_PIECE = 128
EPS = 1e-5


def tile_ctcliptext_kernel(tc, emb, gain, offs, out):
    nc = tc.nc
    emb_blocks = emb.rearrange("(p b) s -> p b s", b=BLOCKS)
    out_blocks = out.rearrange("(p b) n -> p b n", b=BLOCKS)
    gain_blocks = gain.rearrange("(p b) o -> p (b o)", b=BLOCKS)

    with (
        tc.tile_pool(name="held", bufs=1) as held,
        tc.tile_pool(name="staged", bufs=BLOCKS * (N // PIECE) + 1) as staged,
        tc.psum_pool(name="flipped", bufs=1) as flipped,
        tc.psum_pool(name="first", bufs=1) as first,
        tc.psum_pool(name="back", bufs=2) as back,
    ):
        raw = [held.tile([P, BLOCKS, P], F32, name=f"raw{w}") for w in range(WORD_BLOCKS)]
        for w in range(WORD_BLOCKS):
            nc.sync.dma_start(raw[w][:], emb_blocks[:, :, w * P : (w + 1) * P])
        offsets = held.tile([P, N // 16], U16, name="offsets")
        nc.sync.dma_start(offsets[:], offs)
        gains = held.tile([P, BLOCKS], F32, name="gains")
        nc.scalar.dma_start(gains[:], gain_blocks)

        identity = held.tile([P, P], F32, name="identity")
        make_identity(nc, identity[:])
        eps = held.tile([P, 1], F32, name="eps")
        nc.vector.memset(eps[:], EPS)
        scratch = held.tile([P, 1], F32, name="scratch")
        nc.scalar.activation(scratch[:], eps[:], FUNC.Abs_reciprocal_sqrt)
        gain_wide = [held.tile([P, PIECE], F32, name=f"gain_wide{b}") for b in range(BLOCKS)]
        for b in range(BLOCKS):
            nc.scalar.copy(gain_wide[b][:], gains[:, b : b + 1].to_broadcast([P, PIECE]))

        raw_flipped = [flipped.tile([P, C], F32, name=f"raw_flipped{w}") for w in range(WORD_BLOCKS)]
        for w in range(WORD_BLOCKS):
            for b in range(BLOCKS):
                nc.tensor.transpose(raw_flipped[w][:, b * P : (b + 1) * P], raw[w][:, b, :], identity[:])

        stats = held.tile([P, WORD_BLOCKS, 6], F32, name="stats")
        mean_var = held.tile([P, WORD_BLOCKS, 2], F32, name="mean_var")
        rstd = held.tile([P, WORD_BLOCKS], F32, name="rstd")

        def measure(w):
            nc.vector.bn_stats(stats[:, w, :], raw_flipped[w][:])
            nc.vector.bn_aggr(mean_var[:, w, :], stats[:, w, :])
            nc.scalar.activation(rstd[:, w : w + 1], mean_var[:, w, 1:2], FUNC.Abs_reciprocal_sqrt, bias=eps[:])

        z = [held.tile([P, S], F32, name=f"z{b}") for b in range(BLOCKS)]

        first_flipped = held.tile([P, WORD_BLOCKS, P], F32, name="first_flipped")
        EARLY = (WORD_BLOCKS - 1) * P
        early_psum = first.tile([P, EARLY], F32, name="early_psum")
        last_psum = first.tile([P, P], F32, name="last_psum")

        def normalise_first(w):
            nc.vector.tensor_scalar(
                first_flipped[:, w, :], raw_flipped[w][:, 0:P],
                mean_var[:, w, 0:1], rstd[:, w : w + 1], ALU.subtract, ALU.mult,
            )
            back_in_psum = early_psum[:, w * P : (w + 1) * P] if w < WORD_BLOCKS - 1 else last_psum[:]
            nc.tensor.transpose(back_in_psum, first_flipped[:, w, :], identity[:])

        measure(0)
        for w in range(1, WORD_BLOCKS):
            measure(w)
            normalise_first(w - 1)
        normalise_first(WORD_BLOCKS - 1)
        shift = held.tile([P, WORD_BLOCKS], F32, name="shift")
        nc.vector.scalar_tensor_tensor(shift[:], mean_var[:, :, 0], -1.0, rstd[:], ALU.mult, ALU.mult)
        nc.vector.tensor_copy(z[0][:, 0:EARLY], early_psum[:])
        nc.vector.tensor_copy(z[0][:, EARLY:S], last_psum[:])

        rest_flipped = [held.tile([P, C - P], F32, name=f"rest_flipped{w}") for w in range(WORD_BLOCKS)]
        for w in range(WORD_BLOCKS):
            nc.scalar.activation(
                rest_flipped[w][:], raw_flipped[w][:, P:C], FUNC.Identity,
                bias=shift[:, w : w + 1], scale=rstd[:, w : w + 1],
            )
        for b in range(1, BLOCKS):
            z_psum = back.tile([P, S], F32, name="z_psum")
            for w in range(WORD_BLOCKS):
                nc.tensor.transpose(z_psum[:, w * P : (w + 1) * P], rest_flipped[w][:, (b - 1) * P : b * P], identity[:])
            nc.scalar.copy(z[b][:], z_psum[:])

        for b in range(BLOCKS):
            cuts = list(range(0, N + 1, PIECE))
            if b == BLOCKS - 1:
                cuts.insert(len(cuts) - 1, N - LAST_PIECE)
            for k in range(len(cuts) - 1):
                start, width = cuts[k], cuts[k + 1] - cuts[k]
                picked = staged.tile([P, PIECE], F32, name="picked")
                nc.vector.tensor_tensor(
                    picked[:, 0:width],
                    z[b][:].indirect(offsets[:, start // 16 : (start + width) // 16]),
                    gain_wide[b][:, 0:width],
                    ALU.mult,
                )
                nc.sync.dma_start(out_blocks[:, b, start : start + width], picked[:, 0:width])
